import numpy as np
import ml_dtypes

BF16 = ml_dtypes.bfloat16


def bf(x):
    return np.asarray(x, np.float32).astype(BF16)


def f32(x):
    return np.asarray(x, np.float32)


def f64(x):
    return np.asarray(x).astype(np.float64)


def striped(idx):
    return np.tile(idx.reshape(-1, 16).T, (8, 1))


C, V, NB, LEN0, LEN1, LEN2, LEN3, N = 256, 2048, 8, 1, 5, 10, 16, 256
LENS = (LEN0, LEN1, LEN2, LEN3)
assert N == NB * sum(LENS)


def setup_inputs():
    table = f32(np.random.standard_normal((C, V)))
    wgt = f32(np.concatenate([np.full(NB * n, 1.0 / n) for n in LENS])[None, :])
    idx = np.random.permutation(np.tile(np.arange(V), 2))[:N]
    return {"table": table, "wgt": wgt, "offs": striped(idx)}


def reference(table, wgt, offs):
    idx = offs[:16].T.reshape(-1)
    prod = f64(table)[:, idx] * f64(wgt)
    cols = []
    start = 0
    for n in LENS:
        cols.append(prod[:, start:start + NB * n].reshape(C, NB, n).sum(axis=2))
        start += NB * n
    return np.concatenate(cols, axis=1)

@@ -1,0 +1,53 @@
+import concourse.mybir as mybir
+
+P = 128
+FEATURES, SYMBOLS, ENTRIES = 256, 2048, 256
+STEPS = 8
+SLOT_LENGTHS = (1, 5, 10, 16)
+F32, U16 = mybir.dt.float32, mybir.dt.uint16
+MULT, ADD = mybir.AluOpType.mult, mybir.AluOpType.add
+
+assert STEPS * sum(SLOT_LENGTHS) == ENTRIES
+
+
+def tile_actions_emb_kernel(tc, table, wgt, offs, out):
+    nc = tc.nc
+    blocks = FEATURES // P
+    with (
+        tc.tile_pool(name="held", bufs=1) as held,
+        tc.tile_pool(name="work", bufs=2) as work,
+    ):
+        offsets = held.tile([P, ENTRIES // 16], U16, name="offsets")
+        nc.sync.dma_start(offsets[:], offs)
+
+        weights = held.tile([P, ENTRIES], F32, name="weights")
+        nc.scalar.dma_start(weights[:], wgt.broadcast_to([P, ENTRIES]))
+
+        windows = []
+        for b in range(blocks):
+            window = held.tile([P, SYMBOLS], F32, name=f"window{b}")
+            nc.sync.dma_start(window[:], table[b * P : (b + 1) * P, :])
+            windows.append(window)
+
+        for b in range(blocks):
+            weighted = work.tile([P, ENTRIES], F32, name="weighted")
+            nc.vector.tensor_tensor(
+                weighted[:], windows[b][:].indirect(offsets[:]), weights[:], MULT
+            )
+
+            slots = work.tile([P, len(SLOT_LENGTHS) * STEPS], F32, name="slots")
+            start = 0
+            for q, length in enumerate(SLOT_LENGTHS):
+                entries = weighted[:, start : start + STEPS * length]
+                sums = slots[:, q * STEPS : (q + 1) * STEPS]
+                if length == 1:
+                    nc.vector.tensor_copy(sums, entries)
+                else:
+                    nc.vector.tensor_reduce(
+                        sums,
+                        entries.rearrange("p (r l) -> p r l", l=length),
+                        mybir.AxisListType.X,
+                        ADD,
+                    )
+                start += STEPS * length
+            nc.sync.dma_start(out[b * P : (b + 1) * P, :], slots[:])

@@ -21,12 +21,12 @@ def tile_actions_emb_kernel(tc, table, wgt, offs, out):
         nc.sync.dma_start(offsets[:], offs)
 
         weights = held.tile([P, ENTRIES], F32, name="weights")
-        nc.scalar.dma_start(weights[:], wgt.broadcast_to([P, ENTRIES]))
+        nc.sync.dma_start(weights[:], wgt.broadcast_to([P, ENTRIES]))
 
         windows = []
         for b in range(blocks):
             window = held.tile([P, SYMBOLS], F32, name=f"window{b}")
-            nc.sync.dma_start(window[:], table[b * P : (b + 1) * P, :])
+            nc.scalar.dma_start(window[:], table[b * P : (b + 1) * P, :])
             windows.append(window)
 
         for b in range(blocks):

@@ -16,12 +16,19 @@ def tile_actions_emb_kernel(tc, table, wgt, offs, out):
     with (
         tc.tile_pool(name="held", bufs=1) as held,
         tc.tile_pool(name="work", bufs=2) as work,
+        tc.psum_pool(name="psum", bufs=1) as psum,
     ):
         offsets = held.tile([P, ENTRIES // 16], U16, name="offsets")
         nc.sync.dma_start(offsets[:], offs)
 
+        weights_row = held.tile([1, ENTRIES], F32, name="weights_row")
+        nc.sync.dma_start(weights_row[:], wgt)
+        ones = held.tile([1, P], F32, name="ones")
+        nc.vector.memset(ones[:], 1.0)
+        repeated = psum.tile([P, ENTRIES], F32, name="repeated")
+        nc.tensor.matmul(repeated[:], ones[:], weights_row[:], start=True, stop=True)
         weights = held.tile([P, ENTRIES], F32, name="weights")
-        nc.sync.dma_start(weights[:], wgt.broadcast_to([P, ENTRIES]))
+        nc.vector.tensor_copy(weights[:], repeated[:])
 
         windows = []
         for b in range(blocks):

@@ -18,11 +18,12 @@ def tile_actions_emb_kernel(tc, table, wgt, offs, out):
         tc.tile_pool(name="work", bufs=2) as work,
         tc.psum_pool(name="psum", bufs=1) as psum,
     ):
+        weights_row = held.tile([1, ENTRIES], F32, name="weights_row")
+        nc.sync.dma_start(weights_row[:], wgt)
+
         offsets = held.tile([P, ENTRIES // 16], U16, name="offsets")
         nc.sync.dma_start(offsets[:], offs)
 
-        weights_row = held.tile([1, ENTRIES], F32, name="weights_row")
-        nc.sync.dma_start(weights_row[:], wgt)
         ones = held.tile([1, P], F32, name="ones")
         nc.vector.memset(ones[:], 1.0)
         repeated = psum.tile([P, ENTRIES], F32, name="repeated")

@@ -1,6 +1,7 @@
 import concourse.mybir as mybir
 
 P = 128
+HALF = P // 2
 FEATURES, SYMBOLS, ENTRIES = 256, 2048, 256
 STEPS = 8
 SLOT_LENGTHS = (1, 5, 10, 16)
@@ -58,4 +59,6 @@ def tile_actions_emb_kernel(tc, table, wgt, offs, out):
                         ADD,
                     )
                 start += STEPS * length
-            nc.sync.dma_start(out[b * P : (b + 1) * P, :], slots[:])
+
+            nc.sync.dma_start(out[b * P : b * P + HALF, :], slots[:HALF, :])
+            nc.scalar.dma_start(out[b * P + HALF : (b + 1) * P, :], slots[HALF:, :])

@@ -1,7 +1,6 @@
 import concourse.mybir as mybir
 
 P = 128
-HALF = P // 2
 FEATURES, SYMBOLS, ENTRIES = 256, 2048, 256
 STEPS = 8
 SLOT_LENGTHS = (1, 5, 10, 16)
@@ -60,5 +59,5 @@ def tile_actions_emb_kernel(tc, table, wgt, offs, out):
                     )
                 start += STEPS * length
 
-            nc.sync.dma_start(out[b * P : b * P + HALF, :], slots[:HALF, :])
-            nc.scalar.dma_start(out[b * P + HALF : (b + 1) * P, :], slots[HALF:, :])
+            store_queue = nc.sync if b == blocks - 1 else nc.scalar
+            store_queue.dma_start(out[b * P : (b + 1) * P, :], slots[:])

@@ -8,6 +8,8 @@ F32, U16 = mybir.dt.float32, mybir.dt.uint16
 MULT, ADD = mybir.AluOpType.mult, mybir.AluOpType.add
 
 assert STEPS * sum(SLOT_LENGTHS) == ENTRIES
+HALF = ENTRIES // 2
+assert STEPS * sum(SLOT_LENGTHS[:-1]) == HALF
 
 
 def tile_actions_emb_kernel(tc, table, wgt, offs, out):
@@ -38,15 +40,22 @@ def tile_actions_emb_kernel(tc, table, wgt, offs, out):
             windows.append(window)
 
         for b in range(blocks):
-            weighted = work.tile([P, ENTRIES], F32, name="weighted")
-            nc.vector.tensor_tensor(
-                weighted[:], windows[b][:].indirect(offsets[:]), weights[:], MULT
-            )
+            weighted = []
+            for h in range(2):
+                half = work.tile([P, HALF], F32, name=f"weighted{h}")
+                nc.vector.tensor_tensor(
+                    half[:],
+                    windows[b][:].indirect(offsets[:, h * HALF // 16 : (h + 1) * HALF // 16]),
+                    weights[:, h * HALF : (h + 1) * HALF],
+                    MULT,
+                )
+                weighted.append(half)
 
             slots = work.tile([P, len(SLOT_LENGTHS) * STEPS], F32, name="slots")
             start = 0
             for q, length in enumerate(SLOT_LENGTHS):
-                entries = weighted[:, start : start + STEPS * length]
+                first = start % HALF
+                entries = weighted[start // HALF][:, first : first + STEPS * length]
                 sums = slots[:, q * STEPS : (q + 1) * STEPS]
                 if length == 1:
                     nc.vector.tensor_copy(sums, entries)

@@ -39,6 +39,7 @@ def tile_actions_emb_kernel(tc, table, wgt, offs, out):
             nc.scalar.dma_start(window[:], table[b * P : (b + 1) * P, :])
             windows.append(window)
 
+        slots = held.tile([P, blocks, len(SLOT_LENGTHS) * STEPS], F32, name="slots")
         for b in range(blocks):
             weighted = []
             for h in range(2):
@@ -51,12 +52,11 @@ def tile_actions_emb_kernel(tc, table, wgt, offs, out):
                 )
                 weighted.append(half)
 
-            slots = work.tile([P, len(SLOT_LENGTHS) * STEPS], F32, name="slots")
             start = 0
             for q, length in enumerate(SLOT_LENGTHS):
                 first = start % HALF
                 entries = weighted[start // HALF][:, first : first + STEPS * length]
-                sums = slots[:, q * STEPS : (q + 1) * STEPS]
+                sums = slots[:, b, q * STEPS : (q + 1) * STEPS]
                 if length == 1:
                     nc.vector.tensor_copy(sums, entries)
                 else:
@@ -68,5 +68,4 @@ def tile_actions_emb_kernel(tc, table, wgt, offs, out):
                     )
                 start += STEPS * length
 
-            store_queue = nc.sync if b == blocks - 1 else nc.scalar
-            store_queue.dma_start(out[b * P : (b + 1) * P, :], slots[:])
+        nc.sync.dma_start(out.rearrange("(b p) s -> p b s", p=P), slots[:])

@@ -33,10 +33,11 @@ def tile_actions_emb_kernel(tc, table, wgt, offs, out):
         weights = held.tile([P, ENTRIES], F32, name="weights")
         nc.vector.tensor_copy(weights[:], repeated[:])
 
+        table_by_block = table.rearrange("(p b) v -> p b v", b=blocks)
         windows = []
         for b in range(blocks):
             window = held.tile([P, SYMBOLS], F32, name=f"window{b}")
-            nc.scalar.dma_start(window[:], table[b * P : (b + 1) * P, :])
+            nc.scalar.dma_start(window[:], table_by_block[:, b, :])
             windows.append(window)
 
         slots = held.tile([P, blocks, len(SLOT_LENGTHS) * STEPS], F32, name="slots")
@@ -68,4 +69,4 @@ def tile_actions_emb_kernel(tc, table, wgt, offs, out):
                     )
                 start += STEPS * length
 
-        nc.sync.dma_start(out.rearrange("(b p) s -> p b s", p=P), slots[:])
+        nc.sync.dma_start(out.rearrange("(p b) s -> p b s", b=blocks), slots[:])

@@ -4,6 +4,7 @@ P = 128
 FEATURES, SYMBOLS, ENTRIES = 256, 2048, 256
 STEPS = 8
 SLOT_LENGTHS = (1, 5, 10, 16)
+DMA_BURST = 256
 F32, U16 = mybir.dt.float32, mybir.dt.uint16
 MULT, ADD = mybir.AluOpType.mult, mybir.AluOpType.add
 
@@ -36,11 +37,13 @@ def tile_actions_emb_kernel(tc, table, wgt, offs, out):
         table_by_block = table.rearrange("(p b) v -> p b v", b=blocks)
         windows = []
         for b in range(blocks):
-            window = held.tile([P, SYMBOLS], F32, name=f"window{b}")
+            window = held.tile([P, SYMBOLS], F32, name=f"window{b}", align_bytes=DMA_BURST)
             nc.scalar.dma_start(window[:], table_by_block[:, b, :])
             windows.append(window)
 
-        slots = held.tile([P, blocks, len(SLOT_LENGTHS) * STEPS], F32, name="slots")
+        slots = held.tile(
+            [P, blocks, len(SLOT_LENGTHS) * STEPS], F32, name="slots", align_bytes=DMA_BURST
+        )
         for b in range(blocks):
             weighted = []
             for h in range(2):

@@ -21,25 +21,29 @@ def tile_actions_emb_kernel(tc, table, wgt, offs, out):
         tc.tile_pool(name="work", bufs=2) as work,
         tc.psum_pool(name="psum", bufs=1) as psum,
     ):
-        weights_row = held.tile([1, ENTRIES], F32, name="weights_row")
-        nc.sync.dma_start(weights_row[:], wgt)
-
-        offsets = held.tile([P, ENTRIES // 16], U16, name="offsets")
-        nc.sync.dma_start(offsets[:], offs)
-
-        ones = held.tile([1, P], F32, name="ones")
-        nc.vector.memset(ones[:], 1.0)
-        repeated = psum.tile([P, ENTRIES], F32, name="repeated")
-        nc.tensor.matmul(repeated[:], ones[:], weights_row[:], start=True, stop=True)
-        weights = held.tile([P, ENTRIES], F32, name="weights")
-        nc.vector.tensor_copy(weights[:], repeated[:])
-
         table_by_block = table.rearrange("(p b) v -> p b v", b=blocks)
         windows = []
         for b in range(blocks):
             window = held.tile([P, SYMBOLS], F32, name=f"window{b}", align_bytes=DMA_BURST)
-            nc.scalar.dma_start(window[:], table_by_block[:, b, :])
             windows.append(window)
+        offsets = held.tile([P, ENTRIES // 16], U16, name="offsets")
+        weights_row = held.tile([1, ENTRIES], F32, name="weights_row")
+        nc.sync.dma_start(windows[0][:], table_by_block[:, 0, :])
+        nc.scalar.dma_start(weights_row[:], wgt)
+        nc.sync.dma_start(offsets[:], offs)
+        nc.sync.dma_start(windows[1][:], table_by_block[:, 1, :])
+
+        ones = held.tile([1, P], F32, name="ones")
+        nc.vector.memset(ones[:], 1.0)
+        weights = []
+        for h in range(2):
+            repeated = psum.tile([P, HALF], F32, name=f"repeated{h}")
+            nc.tensor.matmul(
+                repeated[:], ones[:], weights_row[:, h * HALF : (h + 1) * HALF], start=True, stop=True
+            )
+            half_weights = held.tile([P, HALF], F32, name=f"weights{h}")
+            nc.vector.tensor_copy(half_weights[:], repeated[:])
+            weights.append(half_weights)
 
         slots = held.tile(
             [P, blocks, len(SLOT_LENGTHS) * STEPS], F32, name="slots", align_bytes=DMA_BURST
@@ -51,7 +55,7 @@ def tile_actions_emb_kernel(tc, table, wgt, offs, out):
                 nc.vector.tensor_tensor(
                     half[:],
                     windows[b][:].indirect(offsets[:, h * HALF // 16 : (h + 1) * HALF // 16]),
-                    weights[:, h * HALF : (h + 1) * HALF],
+                    weights[h][:],
                     MULT,
                 )
                 weighted.append(half)

import concourse.mybir as mybir

P = 128
FEATURES, SYMBOLS, ENTRIES = 256, 2048, 256
STEPS = 8
SLOT_LENGTHS = (1, 5, 10, 16)
DMA_BURST = 256
F32, U16 = mybir.dt.float32, mybir.dt.uint16
MULT, ADD = mybir.AluOpType.mult, mybir.AluOpType.add

assert STEPS * sum(SLOT_LENGTHS) == ENTRIES
HALF = ENTRIES // 2
assert STEPS * sum(SLOT_LENGTHS[:-1]) == HALF


def tile_actions_emb_kernel(tc, table, wgt, offs, out):
    nc = tc.nc
    blocks = FEATURES // P
    with (
        tc.tile_pool(name="held", bufs=1) as held,
        tc.tile_pool(name="work", bufs=2) as work,
        tc.psum_pool(name="psum", bufs=1) as psum,
    ):
        table_by_block = table.rearrange("(p b) v -> p b v", b=blocks)
        windows = []
        for b in range(blocks):
            window = held.tile([P, SYMBOLS], F32, name=f"window{b}", align_bytes=DMA_BURST)
            windows.append(window)
        offsets = held.tile([P, ENTRIES // 16], U16, name="offsets")
        weights_row = held.tile([1, ENTRIES], F32, name="weights_row")
        nc.sync.dma_start(windows[0][:], table_by_block[:, 0, :])
        nc.scalar.dma_start(weights_row[:], wgt)
        nc.sync.dma_start(offsets[:], offs)
        nc.sync.dma_start(windows[1][:], table_by_block[:, 1, :])

        ones = held.tile([1, P], F32, name="ones")
        nc.vector.memset(ones[:], 1.0)
        weights = []
        for h in range(2):
            repeated = psum.tile([P, HALF], F32, name=f"repeated{h}")
            nc.tensor.matmul(
                repeated[:], ones[:], weights_row[:, h * HALF : (h + 1) * HALF], start=True, stop=True
            )
            half_weights = held.tile([P, HALF], F32, name=f"weights{h}")
            nc.vector.tensor_copy(half_weights[:], repeated[:])
            weights.append(half_weights)

        slots = held.tile(
            [P, blocks, len(SLOT_LENGTHS) * STEPS], F32, name="slots", align_bytes=DMA_BURST
        )
        for b in range(blocks):
            weighted = []
            for h in range(2):
                half = work.tile([P, HALF], F32, name=f"weighted{h}")
                nc.vector.tensor_tensor(
                    half[:],
                    windows[b][:].indirect(offsets[:, h * HALF // 16 : (h + 1) * HALF // 16]),
                    weights[h][:],
                    MULT,
                )
                weighted.append(half)

            start = 0
            for q, length in enumerate(SLOT_LENGTHS):
                first = start % HALF
                entries = weighted[start // HALF][:, first : first + STEPS * length]
                sums = slots[:, b, q * STEPS : (q + 1) * STEPS]
                if length == 1:
                    nc.vector.tensor_copy(sums, entries)
                else:
                    nc.vector.tensor_reduce(
                        sums,
                        entries.rearrange("p (r l) -> p r l", l=length),
                        mybir.AxisListType.X,
                        ADD,
                    )
                start += STEPS * length

        nc.sync.dma_start(out.rearrange("(p b) s -> p b s", b=blocks), slots[:])
